import numpy as np
import ml_dtypes


def mxq(x, axis, fmt="e4m3"):
    dtype, down = {"e4m3": (ml_dtypes.float8_e4m3fn, 7), "e5m2": (ml_dtypes.float8_e5m2, 14)}[fmt]
    v = np.moveaxis(np.asarray(x, np.float32).astype(ml_dtypes.bfloat16).astype(np.float64), axis, -1)
    blocks = v.reshape(v.shape[:-1] + (-1, 32))
    amax = np.abs(blocks).max(-1, keepdims=True)
    byte = np.maximum(np.where(amax > 0, np.frexp(amax)[1] - 1 + 127, 0) - down, 1)
    scale = np.exp2(byte - 127.0)
    codes = (blocks / scale).astype(np.float32).astype(dtype).astype(np.float64)
    return np.moveaxis((codes * scale).reshape(v.shape), -1, axis)


WIDE = False


def mx_kscale(k):
    if not WIDE:
        return np.ones(k)
    levels = np.array([10, -10, 5, -5, 0])
    a = np.random.permutation(np.resize(levels, k // 512 * 4)).reshape(k // 512, 4)
    idx = np.arange(k)
    return np.exp2(a[idx // 512, idx % 128 // 32])


BF16 = ml_dtypes.bfloat16


def bf(x):
    return np.asarray(x, np.float32).astype(BF16)


def f64(x):
    return np.asarray(x).astype(np.float64)


B, S, D = 2, 512, 1024


def setup_inputs():
    s = mx_kscale(D)
    return {"X": bf(np.random.standard_normal((B, S, D)) * s),
            "Wq": bf(np.random.standard_normal((D, D)) * 2.5 / np.sqrt(D) / s[:, None]),
            "bq": bf(np.random.standard_normal(D) * 0.3),
            "Wv": bf(np.random.standard_normal((D, D)) / np.sqrt(D) / s[:, None]),
            "bv": bf(np.random.standard_normal(D) * 0.3)}


def reference(X, Wq, bq, Wv, bv):
    xq = mxq(f64(X), 2, "e4m3")
    q = (xq @ mxq(f64(Wq), 0, "e4m3")) + f64(bq)
    v = (xq @ mxq(f64(Wv), 0, "e4m3")) + f64(bv)
    v_viewed = np.reshape(v, (B, D, S))
    scores = (mxq(q, 2, "e4m3") @ mxq(v_viewed, 1, "e4m3")) / np.sqrt(D)
    return scores, v

@@ -1,0 +1,241 @@
+import math
+from contextlib import ExitStack
+
+import concourse.mybir as mybir
+from concourse.masks import make_identity
+
+F32 = mybir.dt.float32
+BF16 = mybir.dt.bfloat16
+I32 = mybir.dt.int32
+U32 = mybir.dt.uint32
+U8 = mybir.dt.uint8
+FP8X4 = mybir.dt.float8_e4m3fn_x4
+
+P = 128
+PACK = 4
+K_PASS = P * PACK
+B, S, D = 2, 512, 1024
+PASSES = D // K_PASS
+BANK = 512
+HALVES = D // BANK
+TILES = S // P
+RUN = 4
+
+FLOPS = 2 * (2 * B * S * D * D) + 2 * B * S * S * D
+
+
+def tile_selfattention_pa_kernel(tc, X, Wq, bq, Wv, bv, out_0, out_1):
+    nc = tc.nc
+    with ExitStack() as ctx:
+        keep = ctx.enter_context(tc.tile_pool(name="keep", bufs=1))
+        w_stage = ctx.enter_context(tc.tile_pool(name="w_stage", bufs=4))
+        v_stage = ctx.enter_context(tc.tile_pool(name="v_stage", bufs=2))
+        q_stage = ctx.enter_context(tc.tile_pool(name="q_stage", bufs=2))
+        results = ctx.enter_context(tc.tile_pool(name="results", bufs=4))
+        psum = ctx.enter_context(tc.psum_pool(name="psum", bufs=8))
+
+        x_raw = [[None] * PASSES for b in range(B)]
+        w_raw = {}
+
+        def load_tokens(b):
+            for g in range(PASSES):
+                rows = keep.tile([P, 2, D], BF16, name="x_raw_%d_%d" % (b, g))
+                nc.sync.dma_start(
+                    out=rows[:].rearrange("p u k -> p (u k)"),
+                    in_=X[b, 2 * P * g : 2 * P * (g + 1), :].rearrange("(p u) k -> p (u k)", u=2),
+                )
+                x_raw[b][g] = rows
+
+        def load_weight(label, W):
+            w_raw[label] = []
+            for kp in range(PASSES):
+                rows = keep.tile([P, PACK, D], BF16, name="w_raw_%s_%d" % (label, kp))
+                nc.sync.dma_start(
+                    out=rows[:].rearrange("p (u e) n -> p u (e n)", u=2),
+                    in_=W[K_PASS * kp : K_PASS * (kp + 1), :].rearrange(
+                        "(u p e) n -> p u (e n)", u=2, e=2
+                    ),
+                )
+                w_raw[label].append(rows)
+
+        load_tokens(0)
+        load_weight("v", Wv)
+        load_tokens(1)
+        load_weight("q", Wq)
+
+        identity = keep.tile([P, P], F32, name="identity")
+        make_identity(nc, identity[:])
+        ones = keep.tile([P, P], BF16, name="ones")
+        nc.vector.memset(ones[:], 1.0)
+        bias_rows = keep.tile([P, 2, D], BF16, name="bias_rows")
+        nc.vector.memset(bias_rows[:].bitcast(I32), 0)
+        nc.scalar.dma_start(out=bias_rows[0:1, 0, :], in_=bq.rearrange("(o n) -> o n", o=1))
+        nc.scalar.dma_start(out=bias_rows[0:1, 1, :], in_=bv.rearrange("(o n) -> o n", o=1))
+
+        x_codes = [keep.tile([P, PASSES, S], U32, name="x_codes_%d" % b, align_bytes=64) for b in range(B)]
+        x_scales = [keep.tile([P, PASSES, S], U8, name="x_scales_%d" % b, align_bytes=64) for b in range(B)]
+
+        def prepare_tokens(b):
+            grouped = keep.tile([P, PASSES, S, PACK], BF16, name="x_grouped_%d" % b, align_bytes=64)
+            grouped_words = grouped[:].bitcast(F32)
+            for g in range(PASSES):
+                words = x_raw[b][g][:].bitcast(F32)
+                for u in range(2):
+                    flipped = psum.tile([P, PASSES, 2, P], F32, tag="bank")
+                    for kp in range(PASSES):
+                        for ku in range(2):
+                            first = (2 * kp + ku) * P
+                            nc.tensor.transpose(
+                                flipped[:, kp, ku, :], words[:, u, first : first + P], identity[:]
+                            )
+                    column = (2 * g + u) * P
+                    nc.scalar.copy(
+                        out=grouped_words[:, :, column : column + P, :],
+                        in_=flipped[:].rearrange("p a u c -> p a c u"),
+                    )
+            for kp in range(PASSES):
+                nc.vector.quantize_mx(
+                    out=x_codes[b][:, kp, :].bitcast(FP8X4),
+                    scales=x_scales[b][:, kp, :],
+                    in_=grouped[:, kp, :, :].rearrange("p c t -> p (c t)"),
+                )
+
+        def regroup(copy, grouped_view, rows):
+            copy(out=grouped_view, in_=rows.rearrange("p t (c i) -> p c t i", i=RUN))
+
+        def prepare_weight(label, column_order):
+            codes = keep.tile([P, PASSES, D], U32, name="w_codes_%s" % label, align_bytes=64)
+            scales = keep.tile([P, PASSES, D], U8, name="w_scales_%s" % label, align_bytes=64)
+            for kp in range(PASSES):
+                grouped = []
+                for half in range(HALVES):
+                    w_grouped = w_stage.tile([P, BANK, PACK], BF16, align_bytes=64)
+                    regroup(
+                        nc.vector.tensor_copy if half == 0 else nc.scalar.copy,
+                        w_grouped[:].rearrange(column_order, i=RUN),
+                        w_raw[label][kp][:, :, BANK * half : BANK * (half + 1)],
+                    )
+                    grouped.append(w_grouped)
+                for half in range(HALVES):
+                    columns = slice(BANK * half, BANK * (half + 1))
+                    nc.vector.quantize_mx(
+                        out=codes[:, kp, columns].bitcast(FP8X4),
+                        scales=scales[:, kp, columns],
+                        in_=grouped[half][:].rearrange("p c t -> p (c t)"),
+                    )
+            return codes, scales
+
+        bv_all = keep.tile([P, HALVES, BANK], F32, name="bv_all")
+        bq_column = keep.tile([P, PASSES * PACK], F32, name="bq_column")
+
+        def spread_biases():
+            for h in range(HALVES):
+                spread = psum.tile([P, BANK], F32, tag="bank")
+                nc.tensor.matmul(
+                    out=spread[:], lhsT=ones[:], rhs=bias_rows[:, 1, BANK * h : BANK * (h + 1)],
+                    start=True, stop=True,
+                )
+                nc.scalar.copy(out=bv_all[:, h, :], in_=spread[:])
+            sorted_bq = bias_rows[:, 0, :].rearrange("p (g q t) -> p g t q", g=PASSES, t=PACK)
+            stood_up = psum.tile([P, PASSES * PACK, 32], F32, tag="bank")
+            for g in range(PASSES):
+                for t in range(PACK):
+                    nc.tensor.matmul(
+                        out=stood_up[:, PACK * g + t, :], lhsT=sorted_bq[:, g, t, :], rhs=ones[:, 0:32],
+                        start=True, stop=True,
+                    )
+            nc.vector.tensor_copy(out=bq_column[:], in_=stood_up[:, :, 0])
+
+        v_codes = [keep.tile([P, PASSES, S], U32, name="v_codes_%d" % b, align_bytes=64) for b in range(B)]
+        v_scales = [keep.tile([P, PASSES, S], U8, name="v_scales_%d" % b, align_bytes=64) for b in range(B)]
+        q_codes = [keep.tile([P, PASSES, S], U32, name="q_codes_%d" % b, align_bytes=64) for b in range(B)]
+        q_scales = [keep.tile([P, PASSES, S], U8, name="q_scales_%d" % b, align_bytes=64) for b in range(B)]
+
+        def mx_group(acc, lhs_codes, lhs_scales, lhs_columns, rhs_codes, rhs_scales, rhs_columns):
+            for kp in range(PASSES):
+                nc.tensor.matmul_mx(
+                    out=acc,
+                    lhsT=lhs_codes[:, kp, lhs_columns].bitcast(FP8X4),
+                    lhsT_scale=lhs_scales[:, kp, lhs_columns],
+                    rhs=rhs_codes[:, kp, rhs_columns].bitcast(FP8X4),
+                    rhs_scale=rhs_scales[:, kp, rhs_columns],
+                    start=(kp == 0),
+                    stop=(kp == PASSES - 1),
+                )
+
+        def project_values(b, g):
+            v_rows = results.tile([P, 2, D], F32)
+            for u in range(2):
+                tokens = slice((2 * g + u) * P, (2 * g + u + 1) * P)
+                for h in range(HALVES):
+                    columns = slice(BANK * h, BANK * (h + 1))
+                    acc = psum.tile([P, BANK], F32, tag="bank")
+                    mx_group(acc[:], x_codes[b], x_scales[b], tokens, wv_codes, wv_scales, columns)
+                    nc.vector.tensor_tensor(
+                        out=v_rows[:, u, columns], in0=acc[:], in1=bv_all[:, h, :], op=mybir.AluOpType.add
+                    )
+            nc.sync.dma_start(
+                out=out_1[b, 2 * P * g : 2 * P * (g + 1), :].rearrange("(p u) n -> p (u n)", u=2),
+                in_=v_rows[:].rearrange("p u n -> p (u n)"),
+            )
+            v_grouped = v_stage.tile([P, BANK, PACK], BF16, align_bytes=64)
+            regroup(
+                nc.scalar.copy,
+                v_grouped[:].rearrange("p (c i) t -> p c t i", i=RUN),
+                v_rows[:].rearrange("p u (h j) -> p (u h) j", h=HALVES),
+            )
+            nc.vector.quantize_mx(
+                out=v_codes[b][:, g, :].bitcast(FP8X4),
+                scales=v_scales[b][:, g, :],
+                in_=v_grouped[:].rearrange("p c t -> p (c t)"),
+            )
+
+        def project_queries(b, g):
+            q_planes = q_stage.tile([P, PACK, S], BF16)
+            for t in range(PACK):
+                features = slice(K_PASS * g + P * t, K_PASS * g + P * (t + 1))
+                acc = psum.tile([P, BANK], F32, tag="bank")
+                mx_group(acc[:], wq_codes, wq_scales, features, x_codes[b], x_scales[b], slice(0, S))
+                nc.scalar.activation(
+                    out=q_planes[:, t, :], in_=acc[:], func=mybir.ActivationFunctionType.Identity,
+                    bias=bq_column[:, PACK * g + t : PACK * g + t + 1], scale=1.0,
+                )
+            q_grouped = q_stage.tile([P, S, PACK], BF16, align_bytes=64)
+            regroup(nc.vector.tensor_copy, q_grouped[:].rearrange("p (c i) t -> p c t i", i=RUN), q_planes[:])
+            nc.vector.quantize_mx(
+                out=q_codes[b][:, g, :].bitcast(FP8X4),
+                scales=q_scales[b][:, g, :],
+                in_=q_grouped[:].rearrange("p c t -> p (c t)"),
+            )
+
+        def score(b):
+            for g in range(PASSES):
+                score_rows = results.tile([P, 2, S], F32)
+                for u in range(2):
+                    tokens = slice((2 * g + u) * P, (2 * g + u + 1) * P)
+                    acc = psum.tile([P, BANK], F32, tag="bank")
+                    mx_group(acc[:], q_codes[b], q_scales[b], tokens, v_codes[b], v_scales[b], slice(0, S))
+                    if u == 0:
+                        nc.scalar.mul(out=score_rows[:, u, :], in_=acc[:], mul=1.0 / math.sqrt(D))
+                    else:
+                        nc.vector.tensor_scalar_mul(out=score_rows[:, u, :], in0=acc[:], scalar1=1.0 / math.sqrt(D))
+                nc.sync.dma_start(
+                    out=out_0[b, 2 * P * g : 2 * P * (g + 1), :].rearrange("(p u) j -> p (u j)", u=2),
+                    in_=score_rows[:].rearrange("p u j -> p (u j)"),
+                )
+
+        prepare_tokens(0)
+        spread_biases()
+        wv_codes, wv_scales = prepare_weight("v", "p (c i) t -> p c t i")
+        prepare_tokens(1)
+        project_values(0, 0)
+        project_values(0, 1)
+        wq_codes, wq_scales = prepare_weight("q", "p (i c) t -> p c t i")
+        project_queries(0, 0)
+        project_values(1, 0)
+        project_queries(0, 1)
+        project_values(1, 1)
+        score(0)
+        project_queries(1, 0)
+        project_queries(1, 1)
+        score(1)

@@ -18,8 +18,9 @@ B, S, D = 2, 512, 1024
 PASSES = D // K_PASS
 BANK = 512
 HALVES = D // BANK
-TILES = S // P
 RUN = 4
+RUNS = BANK // RUN
+VECTOR_RUNS = 84
 
 FLOPS = 2 * (2 * B * S * D * D) + 2 * B * S * S * D
 
@@ -33,8 +34,17 @@ def tile_selfattention_pa_kernel(tc, X, Wq, bq, Wv, bv, out_0, out_1):
         q_stage = ctx.enter_context(tc.tile_pool(name="q_stage", bufs=2))
         results = ctx.enter_context(tc.tile_pool(name="results", bufs=4))
         psum = ctx.enter_context(tc.psum_pool(name="psum", bufs=8))
+        ctx.enter_context(tc.manual_schedule())
+        identity = keep.tile([P, P], F32, name="identity")
+        make_identity(nc, identity[:])
+        ones = keep.tile([P, P], BF16, name="ones")
+        nc.vector.memset(ones[:], 1.0)
+        bias_rows = keep.tile([P, 2, D], BF16, name="bias_rows")
+        nc.vector.memset(bias_rows[:].bitcast(I32), 0)
+        nc.sync.dma_start(out=bias_rows[0:1, 0, :], in_=bq.rearrange("(o n) -> o n", o=1))
+        nc.sync.dma_start(out=bias_rows[0:1, 1, :], in_=bv.rearrange("(o n) -> o n", o=1))
 
-        x_raw = [[None] * PASSES for b in range(B)]
+        x_raw = {}
         w_raw = {}
 
         def load_tokens(b):
@@ -44,98 +54,88 @@ def tile_selfattention_pa_kernel(tc, X, Wq, bq, Wv, bv, out_0, out_1):
                     out=rows[:].rearrange("p u k -> p (u k)"),
                     in_=X[b, 2 * P * g : 2 * P * (g + 1), :].rearrange("(p u) k -> p (u k)", u=2),
                 )
-                x_raw[b][g] = rows
+                x_raw[(b, g)] = rows
 
-        def load_weight(label, W):
-            w_raw[label] = []
+        def load_weight_half(label, W, half):
             for kp in range(PASSES):
-                rows = keep.tile([P, PACK, D], BF16, name="w_raw_%s_%d" % (label, kp))
+                rows = keep.tile([P, PACK, BANK], BF16, name="w_raw_%s_%d_%d" % (label, half, kp))
                 nc.sync.dma_start(
-                    out=rows[:].rearrange("p (u e) n -> p u (e n)", u=2),
-                    in_=W[K_PASS * kp : K_PASS * (kp + 1), :].rearrange(
-                        "(u p e) n -> p u (e n)", u=2, e=2
+                    out=rows[:],
+                    in_=W[K_PASS * kp : K_PASS * (kp + 1), BANK * half : BANK * (half + 1)].rearrange(
+                        "(p t) n -> p t n", t=PACK
                     ),
                 )
-                w_raw[label].append(rows)
+                w_raw[(label, half, kp)] = rows
 
+        load_weight_half("q", Wq, 0)
         load_tokens(0)
-        load_weight("v", Wv)
+        load_weight_half("q", Wq, 1)
+        load_weight_half("v", Wv, 0)
+        load_weight_half("v", Wv, 1)
         load_tokens(1)
-        load_weight("q", Wq)
 
-        identity = keep.tile([P, P], F32, name="identity")
-        make_identity(nc, identity[:])
-        ones = keep.tile([P, P], BF16, name="ones")
-        nc.vector.memset(ones[:], 1.0)
-        bias_rows = keep.tile([P, 2, D], BF16, name="bias_rows")
-        nc.vector.memset(bias_rows[:].bitcast(I32), 0)
-        nc.scalar.dma_start(out=bias_rows[0:1, 0, :], in_=bq.rearrange("(o n) -> o n", o=1))
-        nc.scalar.dma_start(out=bias_rows[0:1, 1, :], in_=bv.rearrange("(o n) -> o n", o=1))
+        def mx_operand(label, columns):
+            codes = keep.tile([P, PASSES, columns], U32, name="%s_codes" % label, align_bytes=64)
+            scales = keep.tile([P, PASSES, columns], U8, name="%s_scales" % label, align_bytes=64)
+            return codes, scales
 
-        x_codes = [keep.tile([P, PASSES, S], U32, name="x_codes_%d" % b, align_bytes=64) for b in range(B)]
-        x_scales = [keep.tile([P, PASSES, S], U8, name="x_scales_%d" % b, align_bytes=64) for b in range(B)]
+        def quantise(operand, kp, columns, grouped):
+            codes, scales = operand
+            nc.vector.quantize_mx(
+                out=codes[:, kp, columns].bitcast(FP8X4),
+                scales=scales[:, kp, columns],
+                in_=grouped.rearrange("p c t -> p (c t)"),
+            )
 
-        def prepare_tokens(b):
-            grouped = keep.tile([P, PASSES, S, PACK], BF16, name="x_grouped_%d" % b, align_bytes=64)
-            grouped_words = grouped[:].bitcast(F32)
+        x_mx = [mx_operand("x%d" % b, S) for b in range(B)]
+
+        x_grouped = [
+            keep.tile([P, PASSES, S, PACK], BF16, name="x_grouped_%d" % b, align_bytes=64) for b in range(B)
+        ]
+
+        def flip_tokens(b):
+            grouped_words = x_grouped[b][:].bitcast(F32)
             for g in range(PASSES):
-                words = x_raw[b][g][:].bitcast(F32)
+                words = x_raw[(b, g)][:].bitcast(F32).rearrange("p u (a q w) -> p u a w q", a=PASSES, w=2)
                 for u in range(2):
                     flipped = psum.tile([P, PASSES, 2, P], F32, tag="bank")
                     for kp in range(PASSES):
-                        for ku in range(2):
-                            first = (2 * kp + ku) * P
-                            nc.tensor.transpose(
-                                flipped[:, kp, ku, :], words[:, u, first : first + P], identity[:]
-                            )
-                    column = (2 * g + u) * P
+                        for w in range(2):
+                            nc.tensor.transpose(flipped[:, kp, w, :], words[:, u, kp, w, :], identity[:])
+                    first = (2 * g + u) * P
                     nc.scalar.copy(
-                        out=grouped_words[:, :, column : column + P, :],
-                        in_=flipped[:].rearrange("p a u c -> p a c u"),
+                        out=grouped_words[:, :, first : first + P, :],
+                        in_=flipped[:].rearrange("p a w c -> p a c w"),
                     )
-            for kp in range(PASSES):
-                nc.vector.quantize_mx(
-                    out=x_codes[b][:, kp, :].bitcast(FP8X4),
-                    scales=x_scales[b][:, kp, :],
-                    in_=grouped[:, kp, :, :].rearrange("p c t -> p (c t)"),
-                )
 
-        def regroup(copy, grouped_view, rows):
-            copy(out=grouped_view, in_=rows.rearrange("p t (c i) -> p c t i", i=RUN))
+        def quantise_tokens(b):
+            for g in range(PASSES):
+                tokens = slice(2 * P * g, 2 * P * (g + 1))
+                for kp in range(PASSES):
+                    quantise(x_mx[b], kp, tokens, x_grouped[b][:, kp, tokens, :])
 
-        def prepare_weight(label, column_order):
-            codes = keep.tile([P, PASSES, D], U32, name="w_codes_%s" % label, align_bytes=64)
-            scales = keep.tile([P, PASSES, D], U8, name="w_scales_%s" % label, align_bytes=64)
+        w_mx = {"q": mx_operand("wq", D), "v": mx_operand("wv", D)}
+        column_order = {"q": "p (i c) t -> p c t i", "v": "p (c i) t -> p c t i"}
+
+        w_grouped_tiles = {}
+
+        def regroup_weight_half(label, half):
             for kp in range(PASSES):
-                grouped = []
-                for half in range(HALVES):
-                    w_grouped = w_stage.tile([P, BANK, PACK], BF16, align_bytes=64)
-                    regroup(
-                        nc.vector.tensor_copy if half == 0 else nc.scalar.copy,
-                        w_grouped[:].rearrange(column_order, i=RUN),
-                        w_raw[label][kp][:, :, BANK * half : BANK * (half + 1)],
-                    )
-                    grouped.append(w_grouped)
-                for half in range(HALVES):
-                    columns = slice(BANK * half, BANK * (half + 1))
-                    nc.vector.quantize_mx(
-                        out=codes[:, kp, columns].bitcast(FP8X4),
-                        scales=scales[:, kp, columns],
-                        in_=grouped[half][:].rearrange("p c t -> p (c t)"),
-                    )
-            return codes, scales
+                w_grouped = w_stage.tile([P, BANK, PACK], BF16, align_bytes=64)
+                source = w_raw[(label, half, kp)][:].rearrange("p t (c i) -> p c t i", i=RUN)
+                target = w_grouped[:].rearrange(column_order[label], i=RUN)
+                nc.vector.tensor_copy(out=target[:, 0:VECTOR_RUNS], in_=source[:, 0:VECTOR_RUNS])
+                nc.scalar.copy(out=target[:, VECTOR_RUNS:RUNS], in_=source[:, VECTOR_RUNS:RUNS])
+                w_grouped_tiles[(label, half, kp)] = w_grouped
+
+        def quantise_weight_half(label, half):
+            for kp in range(PASSES):
+                quantise(w_mx[label], kp, slice(BANK * half, BANK * (half + 1)), w_grouped_tiles[(label, half, kp)][:])
 
         bv_all = keep.tile([P, HALVES, BANK], F32, name="bv_all")
         bq_column = keep.tile([P, PASSES * PACK], F32, name="bq_column")
 
         def spread_biases():
-            for h in range(HALVES):
-                spread = psum.tile([P, BANK], F32, tag="bank")
-                nc.tensor.matmul(
-                    out=spread[:], lhsT=ones[:], rhs=bias_rows[:, 1, BANK * h : BANK * (h + 1)],
-                    start=True, stop=True,
-                )
-                nc.scalar.copy(out=bv_all[:, h, :], in_=spread[:])
             sorted_bq = bias_rows[:, 0, :].rearrange("p (g q t) -> p g t q", g=PASSES, t=PACK)
             stood_up = psum.tile([P, PASSES * PACK, 32], F32, tag="bank")
             for g in range(PASSES):
@@ -145,97 +145,144 @@ def tile_selfattention_pa_kernel(tc, X, Wq, bq, Wv, bv, out_0, out_1):
                         start=True, stop=True,
                     )
             nc.vector.tensor_copy(out=bq_column[:], in_=stood_up[:, :, 0])
-
-        v_codes = [keep.tile([P, PASSES, S], U32, name="v_codes_%d" % b, align_bytes=64) for b in range(B)]
-        v_scales = [keep.tile([P, PASSES, S], U8, name="v_scales_%d" % b, align_bytes=64) for b in range(B)]
-        q_codes = [keep.tile([P, PASSES, S], U32, name="q_codes_%d" % b, align_bytes=64) for b in range(B)]
-        q_scales = [keep.tile([P, PASSES, S], U8, name="q_scales_%d" % b, align_bytes=64) for b in range(B)]
-
-        def mx_group(acc, lhs_codes, lhs_scales, lhs_columns, rhs_codes, rhs_scales, rhs_columns):
-            for kp in range(PASSES):
-                nc.tensor.matmul_mx(
-                    out=acc,
-                    lhsT=lhs_codes[:, kp, lhs_columns].bitcast(FP8X4),
-                    lhsT_scale=lhs_scales[:, kp, lhs_columns],
-                    rhs=rhs_codes[:, kp, rhs_columns].bitcast(FP8X4),
-                    rhs_scale=rhs_scales[:, kp, rhs_columns],
-                    start=(kp == 0),
-                    stop=(kp == PASSES - 1),
+            for h in range(HALVES):
+                spread = psum.tile([P, BANK], F32, tag="bank")
+                nc.tensor.matmul(
+                    out=spread[:], lhsT=ones[:], rhs=bias_rows[:, 1, BANK * h : BANK * (h + 1)],
+                    start=True, stop=True,
                 )
+                nc.scalar.copy(out=bv_all[:, h, :], in_=spread[:])
+
+        v_mx = [mx_operand("v%d" % b, S) for b in range(B)]
+        q_mx = [mx_operand("q%d" % b, S) for b in range(B)]
+
+        def mx_pass(acc, kp, stationary, stationary_columns, moving, moving_columns):
+            nc.tensor.matmul_mx(
+                out=acc,
+                lhsT=stationary[0][:, kp, stationary_columns].bitcast(FP8X4),
+                lhsT_scale=stationary[1][:, kp, stationary_columns],
+                rhs=moving[0][:, kp, moving_columns].bitcast(FP8X4),
+                rhs_scale=moving[1][:, kp, moving_columns],
+                start=(kp == 0),
+                stop=(kp == PASSES - 1),
+            )
+
+        q_planes = {}
+        v_rows = {}
+        score_banks = {}
+        grouped_tiles = {}
+
+        def project_queries(b, g):
+            planes = q_stage.tile([P, PACK, S], BF16, name="q_planes")
+            for t in range(PACK):
+                features = slice(K_PASS * g + P * t, K_PASS * g + P * (t + 1))
+                acc = psum.tile([P, BANK], F32, tag="bank")
+                for kp in range(PASSES):
+                    mx_pass(acc[:], kp, w_mx["q"], features, x_mx[b], slice(0, S))
+                nc.scalar.activation(
+                    out=planes[:, t, :], in_=acc[:], func=mybir.ActivationFunctionType.Identity,
+                    bias=bq_column[:, PACK * g + t : PACK * g + t + 1], scale=1.0,
+                )
+            q_planes[(b, g)] = planes
+
+        def regroup_queries(b, g):
+            q_grouped = q_stage.tile([P, S, PACK], BF16, align_bytes=64)
+            nc.vector.tensor_copy(
+                out=q_grouped[:].rearrange("p (c i) t -> p c t i", i=RUN),
+                in_=q_planes[(b, g)][:].rearrange("p t (c i) -> p c t i", i=RUN),
+            )
+            grouped_tiles[("q", b, g)] = q_grouped
+
+        def quantise_queries(b, g):
+            quantise(q_mx[b], g, slice(0, S), grouped_tiles[("q", b, g)][:])
 
         def project_values(b, g):
-            v_rows = results.tile([P, 2, D], F32)
+            rows = results.tile([P, 2, D], F32, name="v_rows")
             for u in range(2):
                 tokens = slice((2 * g + u) * P, (2 * g + u + 1) * P)
                 for h in range(HALVES):
                     columns = slice(BANK * h, BANK * (h + 1))
                     acc = psum.tile([P, BANK], F32, tag="bank")
-                    mx_group(acc[:], x_codes[b], x_scales[b], tokens, wv_codes, wv_scales, columns)
+                    for kp in range(PASSES):
+                        mx_pass(acc[:], kp, x_mx[b], tokens, w_mx["v"], columns)
                     nc.vector.tensor_tensor(
-                        out=v_rows[:, u, columns], in0=acc[:], in1=bv_all[:, h, :], op=mybir.AluOpType.add
+                        out=rows[:, u, columns], in0=acc[:], in1=bv_all[:, h, :], op=mybir.AluOpType.add
                     )
             nc.sync.dma_start(
                 out=out_1[b, 2 * P * g : 2 * P * (g + 1), :].rearrange("(p u) n -> p (u n)", u=2),
-                in_=v_rows[:].rearrange("p u n -> p (u n)"),
+                in_=rows[:].rearrange("p u n -> p (u n)"),
             )
+            v_rows[(b, g)] = rows
+
+        def regroup_values(b, g):
             v_grouped = v_stage.tile([P, BANK, PACK], BF16, align_bytes=64)
-            regroup(
-                nc.scalar.copy,
-                v_grouped[:].rearrange("p (c i) t -> p c t i", i=RUN),
-                v_rows[:].rearrange("p u (h j) -> p (u h) j", h=HALVES),
+            nc.scalar.copy(
+                out=v_grouped[:].rearrange("p (c i) t -> p c t i", i=RUN),
+                in_=v_rows[(b, g)][:].rearrange("p u (h c i) -> p c (u h) i", h=HALVES, i=RUN),
             )
-            nc.vector.quantize_mx(
-                out=v_codes[b][:, g, :].bitcast(FP8X4),
-                scales=v_scales[b][:, g, :],
-                in_=v_grouped[:].rearrange("p c t -> p (c t)"),
-            )
+            grouped_tiles[("v", b, g)] = v_grouped
 
-        def project_queries(b, g):
-            q_planes = q_stage.tile([P, PACK, S], BF16)
-            for t in range(PACK):
-                features = slice(K_PASS * g + P * t, K_PASS * g + P * (t + 1))
-                acc = psum.tile([P, BANK], F32, tag="bank")
-                mx_group(acc[:], wq_codes, wq_scales, features, x_codes[b], x_scales[b], slice(0, S))
-                nc.scalar.activation(
-                    out=q_planes[:, t, :], in_=acc[:], func=mybir.ActivationFunctionType.Identity,
-                    bias=bq_column[:, PACK * g + t : PACK * g + t + 1], scale=1.0,
-                )
-            q_grouped = q_stage.tile([P, S, PACK], BF16, align_bytes=64)
-            regroup(nc.vector.tensor_copy, q_grouped[:].rearrange("p (c i) t -> p c t i", i=RUN), q_planes[:])
-            nc.vector.quantize_mx(
-                out=q_codes[b][:, g, :].bitcast(FP8X4),
-                scales=q_scales[b][:, g, :],
-                in_=q_grouped[:].rearrange("p c t -> p (c t)"),
-            )
+        def quantise_values(b, g):
+            quantise(v_mx[b], g, slice(0, S), grouped_tiles[("v", b, g)][:])
 
-        def score(b):
+        def add_scores(b, g):
+            if g == 0:
+                score_banks[b] = [psum.tile([P, BANK], F32, tag="bank", name="score_bank") for i in range(S // P)]
+            for i in range(S // P):
+                mx_pass(score_banks[b][i][:], g, q_mx[b], slice(P * i, P * (i + 1)), v_mx[b], slice(0, S))
+
+        def store_scores(b):
             for g in range(PASSES):
                 score_rows = results.tile([P, 2, S], F32)
-                for u in range(2):
-                    tokens = slice((2 * g + u) * P, (2 * g + u + 1) * P)
-                    acc = psum.tile([P, BANK], F32, tag="bank")
-                    mx_group(acc[:], q_codes[b], q_scales[b], tokens, v_codes[b], v_scales[b], slice(0, S))
-                    if u == 0:
-                        nc.scalar.mul(out=score_rows[:, u, :], in_=acc[:], mul=1.0 / math.sqrt(D))
-                    else:
-                        nc.vector.tensor_scalar_mul(out=score_rows[:, u, :], in0=acc[:], scalar1=1.0 / math.sqrt(D))
+                nc.scalar.mul(out=score_rows[:, 0, :], in_=score_banks[b][2 * g][:], mul=1.0 / math.sqrt(D))
+                nc.vector.tensor_scalar_mul(
+                    out=score_rows[:, 1, :], in0=score_banks[b][2 * g + 1][:], scalar1=1.0 / math.sqrt(D)
+                )
                 nc.sync.dma_start(
                     out=out_0[b, 2 * P * g : 2 * P * (g + 1), :].rearrange("(p u) j -> p (u j)", u=2),
                     in_=score_rows[:].rearrange("p u j -> p (u j)"),
                 )
 
-        prepare_tokens(0)
+        regroup_weight_half("q", 0)
+        quantise_weight_half("q", 0)
         spread_biases()
-        wv_codes, wv_scales = prepare_weight("v", "p (c i) t -> p c t i")
-        prepare_tokens(1)
-        project_values(0, 0)
-        project_values(0, 1)
-        wq_codes, wq_scales = prepare_weight("q", "p (i c) t -> p c t i")
+        flip_tokens(0)
+        quantise_tokens(0)
+        regroup_weight_half("q", 1)
+        quantise_weight_half("q", 1)
         project_queries(0, 0)
-        project_values(1, 0)
         project_queries(0, 1)
-        project_values(1, 1)
-        score(0)
+        regroup_weight_half("v", 0)
+        regroup_queries(0, 0)
+        quantise_queries(0, 0)
+        regroup_weight_half("v", 1)
+        regroup_queries(0, 1)
+        quantise_weight_half("v", 0)
+        quantise_queries(0, 1)
+        quantise_weight_half("v", 1)
+        flip_tokens(1)
+        project_values(0, 0)
+        quantise_tokens(1)
+        project_values(0, 1)
+        regroup_values(0, 0)
+        quantise_values(0, 0)
         project_queries(1, 0)
+        project_values(1, 0)
+        regroup_values(0, 1)
+        quantise_values(0, 1)
+        add_scores(0, 0)
+        regroup_queries(1, 0)
+        quantise_queries(1, 0)
         project_queries(1, 1)
-        score(1)
+        add_scores(0, 1)
+        store_scores(0)
+        project_values(1, 1)
+        regroup_values(1, 0)
+        quantise_values(1, 0)
+        regroup_queries(1, 1)
+        quantise_queries(1, 1)
+        add_scores(1, 0)
+        regroup_values(1, 1)
+        quantise_values(1, 1)
+        add_scores(1, 1)
+        store_scores(1)

@@ -41,8 +41,6 @@ def tile_selfattention_pa_kernel(tc, X, Wq, bq, Wv, bv, out_0, out_1):
         nc.vector.memset(ones[:], 1.0)
         bias_rows = keep.tile([P, 2, D], BF16, name="bias_rows")
         nc.vector.memset(bias_rows[:].bitcast(I32), 0)
-        nc.sync.dma_start(out=bias_rows[0:1, 0, :], in_=bq.rearrange("(o n) -> o n", o=1))
-        nc.sync.dma_start(out=bias_rows[0:1, 1, :], in_=bv.rearrange("(o n) -> o n", o=1))
 
         x_raw = {}
         w_raw = {}
@@ -68,6 +66,8 @@ def tile_selfattention_pa_kernel(tc, X, Wq, bq, Wv, bv, out_0, out_1):
                 w_raw[(label, half, kp)] = rows
 
         load_weight_half("q", Wq, 0)
+        nc.sync.dma_start(out=bias_rows[0:1, 0, :], in_=bq.rearrange("(o n) -> o n", o=1))
+        nc.sync.dma_start(out=bias_rows[0:1, 1, :], in_=bv.rearrange("(o n) -> o n", o=1))
         load_tokens(0)
         load_weight_half("q", Wq, 1)
         load_weight_half("v", Wv, 0)
@@ -238,10 +238,9 @@ def tile_selfattention_pa_kernel(tc, X, Wq, bq, Wv, bv, out_0, out_1):
                 nc.vector.tensor_scalar_mul(
                     out=score_rows[:, 1, :], in0=score_banks[b][2 * g + 1][:], scalar1=1.0 / math.sqrt(D)
                 )
-                nc.sync.dma_start(
-                    out=out_0[b, 2 * P * g : 2 * P * (g + 1), :].rearrange("(p u) j -> p (u j)", u=2),
-                    in_=score_rows[:].rearrange("p u j -> p (u j)"),
-                )
+                rows_out = out_0[b, 2 * P * g : 2 * P * (g + 1), :].rearrange("(p u) j -> p u j", u=2)
+                for u in range(2):
+                    nc.sync.dma_start(out=rows_out[:, u, :], in_=score_rows[:, u, :])
 
         regroup_weight_half("q", 0)
         quantise_weight_half("q", 0)
@@ -254,8 +253,8 @@ def tile_selfattention_pa_kernel(tc, X, Wq, bq, Wv, bv, out_0, out_1):
         project_queries(0, 1)
         regroup_weight_half("v", 0)
         regroup_queries(0, 0)
-        quantise_queries(0, 0)
         regroup_weight_half("v", 1)
+        quantise_queries(0, 0)
         regroup_queries(0, 1)
         quantise_weight_half("v", 0)
         quantise_queries(0, 1)
@@ -269,17 +268,17 @@ def tile_selfattention_pa_kernel(tc, X, Wq, bq, Wv, bv, out_0, out_1):
         project_queries(1, 0)
         project_values(1, 0)
         regroup_values(0, 1)
-        quantise_values(0, 1)
-        add_scores(0, 0)
         regroup_queries(1, 0)
+        quantise_values(0, 1)
         quantise_queries(1, 0)
+        add_scores(0, 0)
         project_queries(1, 1)
         add_scores(0, 1)
         store_scores(0)
         project_values(1, 1)
         regroup_values(1, 0)
-        quantise_values(1, 0)
         regroup_queries(1, 1)
+        quantise_values(1, 0)
         quantise_queries(1, 1)
         add_scores(1, 0)
         regroup_values(1, 1)

@@ -6,10 +6,11 @@ from concourse.masks import make_identity
 
 F32 = mybir.dt.float32
 BF16 = mybir.dt.bfloat16
-I32 = mybir.dt.int32
 U32 = mybir.dt.uint32
 U8 = mybir.dt.uint8
 FP8X4 = mybir.dt.float8_e4m3fn_x4
+ADD = mybir.AluOpType.add
+MULT = mybir.AluOpType.mult
 
 P = 128
 PACK = 4
@@ -18,9 +19,9 @@ B, S, D = 2, 512, 1024
 PASSES = D // K_PASS
 BANK = 512
 HALVES = D // BANK
+GROUPS = S // P
 RUN = 4
 RUNS = BANK // RUN
-VECTOR_RUNS = 84
 
 FLOPS = 2 * (2 * B * S * D * D) + 2 * B * S * S * D
 
@@ -29,50 +30,49 @@ def tile_selfattention_pa_kernel(tc, X, Wq, bq, Wv, bv, out_0, out_1):
     nc = tc.nc
     with ExitStack() as ctx:
         keep = ctx.enter_context(tc.tile_pool(name="keep", bufs=1))
-        w_stage = ctx.enter_context(tc.tile_pool(name="w_stage", bufs=4))
-        v_stage = ctx.enter_context(tc.tile_pool(name="v_stage", bufs=2))
-        q_stage = ctx.enter_context(tc.tile_pool(name="q_stage", bufs=2))
-        results = ctx.enter_context(tc.tile_pool(name="results", bufs=4))
         psum = ctx.enter_context(tc.psum_pool(name="psum", bufs=8))
         ctx.enter_context(tc.manual_schedule())
+        bq_cols = keep.tile([P, PASSES, PACK], BF16, name="bq_cols")
+        nc.scalar.dma_start(out=bq_cols[:], in_=bq.rearrange("(g p t) -> p g t", g=PASSES, t=PACK))
+        bv_pairs = keep.tile([P, 4, 2], BF16, name="bv_pairs")
+        nc.scalar.dma_start(out=bv_pairs[:], in_=bv.rearrange("(c p e) -> p c e", c=4, e=2))
         identity = keep.tile([P, P], F32, name="identity")
         make_identity(nc, identity[:])
-        ones = keep.tile([P, P], BF16, name="ones")
-        nc.vector.memset(ones[:], 1.0)
-        bias_rows = keep.tile([P, 2, D], BF16, name="bias_rows")
-        nc.vector.memset(bias_rows[:].bitcast(I32), 0)
 
         x_raw = {}
         w_raw = {}
 
-        def load_tokens(b):
-            for g in range(PASSES):
-                rows = keep.tile([P, 2, D], BF16, name="x_raw_%d_%d" % (b, g))
-                nc.sync.dma_start(
-                    out=rows[:].rearrange("p u k -> p (u k)"),
-                    in_=X[b, 2 * P * g : 2 * P * (g + 1), :].rearrange("(p u) k -> p (u k)", u=2),
-                )
-                x_raw[(b, g)] = rows
+        def load_tokens(b, g):
+            rows = keep.tile([P, 2, D], BF16, name="x_raw_%d_%d" % (b, g))
+            nc.sync.dma_start(
+                out=rows[:].rearrange("p u k -> p (u k)"),
+                in_=X[b, 2 * P * g : 2 * P * (g + 1), :].rearrange("(p u) k -> p (u k)", u=2),
+            )
+            x_raw[(b, g)] = rows
 
-        def load_weight_half(label, W, half):
-            for kp in range(PASSES):
-                rows = keep.tile([P, PACK, BANK], BF16, name="w_raw_%s_%d_%d" % (label, half, kp))
-                nc.sync.dma_start(
-                    out=rows[:],
-                    in_=W[K_PASS * kp : K_PASS * (kp + 1), BANK * half : BANK * (half + 1)].rearrange(
-                        "(p t) n -> p t n", t=PACK
-                    ),
-                )
-                w_raw[(label, half, kp)] = rows
+        def load_weight(label, half, kp):
+            W = Wq if label == "q" else Wv
+            rows = keep.tile([P, PACK, BANK], BF16, name="w_raw_%s_%d_%d" % (label, half, kp))
+            nc.sync.dma_start(
+                out=rows[:],
+                in_=W[K_PASS * kp : K_PASS * (kp + 1), BANK * half : BANK * (half + 1)].rearrange(
+                    "(p t) n -> p t n", t=PACK
+                ),
+            )
+            w_raw[(label, half, kp)] = rows
 
-        load_weight_half("q", Wq, 0)
-        nc.sync.dma_start(out=bias_rows[0:1, 0, :], in_=bq.rearrange("(o n) -> o n", o=1))
-        nc.sync.dma_start(out=bias_rows[0:1, 1, :], in_=bv.rearrange("(o n) -> o n", o=1))
-        load_tokens(0)
-        load_weight_half("q", Wq, 1)
-        load_weight_half("v", Wv, 0)
-        load_weight_half("v", Wv, 1)
-        load_tokens(1)
+        load_weight("v", 0, 0)
+        load_tokens(0, 0)
+        load_weight("v", 0, 1)
+        load_tokens(0, 1)
+        load_weight("v", 1, 0)
+        load_weight("v", 1, 1)
+        load_tokens(1, 0)
+        load_tokens(1, 1)
+        load_weight("q", 0, 0)
+        load_weight("q", 0, 1)
+        load_weight("q", 1, 0)
+        load_weight("q", 1, 1)
 
         def mx_operand(label, columns):
             codes = keep.tile([P, PASSES, columns], U32, name="%s_codes" % label, align_bytes=64)
@@ -87,75 +87,6 @@ def tile_selfattention_pa_kernel(tc, X, Wq, bq, Wv, bv, out_0, out_1):
                 in_=grouped.rearrange("p c t -> p (c t)"),
             )
 
-        x_mx = [mx_operand("x%d" % b, S) for b in range(B)]
-
-        x_grouped = [
-            keep.tile([P, PASSES, S, PACK], BF16, name="x_grouped_%d" % b, align_bytes=64) for b in range(B)
-        ]
-
-        def flip_tokens(b):
-            grouped_words = x_grouped[b][:].bitcast(F32)
-            for g in range(PASSES):
-                words = x_raw[(b, g)][:].bitcast(F32).rearrange("p u (a q w) -> p u a w q", a=PASSES, w=2)
-                for u in range(2):
-                    flipped = psum.tile([P, PASSES, 2, P], F32, tag="bank")
-                    for kp in range(PASSES):
-                        for w in range(2):
-                            nc.tensor.transpose(flipped[:, kp, w, :], words[:, u, kp, w, :], identity[:])
-                    first = (2 * g + u) * P
-                    nc.scalar.copy(
-                        out=grouped_words[:, :, first : first + P, :],
-                        in_=flipped[:].rearrange("p a w c -> p a c w"),
-                    )
-
-        def quantise_tokens(b):
-            for g in range(PASSES):
-                tokens = slice(2 * P * g, 2 * P * (g + 1))
-                for kp in range(PASSES):
-                    quantise(x_mx[b], kp, tokens, x_grouped[b][:, kp, tokens, :])
-
-        w_mx = {"q": mx_operand("wq", D), "v": mx_operand("wv", D)}
-        column_order = {"q": "p (i c) t -> p c t i", "v": "p (c i) t -> p c t i"}
-
-        w_grouped_tiles = {}
-
-        def regroup_weight_half(label, half):
-            for kp in range(PASSES):
-                w_grouped = w_stage.tile([P, BANK, PACK], BF16, align_bytes=64)
-                source = w_raw[(label, half, kp)][:].rearrange("p t (c i) -> p c t i", i=RUN)
-                target = w_grouped[:].rearrange(column_order[label], i=RUN)
-                nc.vector.tensor_copy(out=target[:, 0:VECTOR_RUNS], in_=source[:, 0:VECTOR_RUNS])
-                nc.scalar.copy(out=target[:, VECTOR_RUNS:RUNS], in_=source[:, VECTOR_RUNS:RUNS])
-                w_grouped_tiles[(label, half, kp)] = w_grouped
-
-        def quantise_weight_half(label, half):
-            for kp in range(PASSES):
-                quantise(w_mx[label], kp, slice(BANK * half, BANK * (half + 1)), w_grouped_tiles[(label, half, kp)][:])
-
-        bv_all = keep.tile([P, HALVES, BANK], F32, name="bv_all")
-        bq_column = keep.tile([P, PASSES * PACK], F32, name="bq_column")
-
-        def spread_biases():
-            sorted_bq = bias_rows[:, 0, :].rearrange("p (g q t) -> p g t q", g=PASSES, t=PACK)
-            stood_up = psum.tile([P, PASSES * PACK, 32], F32, tag="bank")
-            for g in range(PASSES):
-                for t in range(PACK):
-                    nc.tensor.matmul(
-                        out=stood_up[:, PACK * g + t, :], lhsT=sorted_bq[:, g, t, :], rhs=ones[:, 0:32],
-                        start=True, stop=True,
-                    )
-            nc.vector.tensor_copy(out=bq_column[:], in_=stood_up[:, :, 0])
-            for h in range(HALVES):
-                spread = psum.tile([P, BANK], F32, tag="bank")
-                nc.tensor.matmul(
-                    out=spread[:], lhsT=ones[:], rhs=bias_rows[:, 1, BANK * h : BANK * (h + 1)],
-                    start=True, stop=True,
-                )
-                nc.scalar.copy(out=bv_all[:, h, :], in_=spread[:])
-
-        v_mx = [mx_operand("v%d" % b, S) for b in range(B)]
-        q_mx = [mx_operand("q%d" % b, S) for b in range(B)]
-
         def mx_pass(acc, kp, stationary, stationary_columns, moving, moving_columns):
             nc.tensor.matmul_mx(
                 out=acc,
@@ -167,121 +98,260 @@ def tile_selfattention_pa_kernel(tc, X, Wq, bq, Wv, bv, out_0, out_1):
                 stop=(kp == PASSES - 1),
             )
 
-        q_planes = {}
-        v_rows = {}
-        score_banks = {}
-        grouped_tiles = {}
+        x_mx = [mx_operand("x%d" % b, S) for b in range(B)]
+        x_grouped = [
+            keep.tile([P, PASSES, S, PACK], BF16, name="x_grouped_%d" % b, align_bytes=64) for b in range(B)
+        ]
 
-        def project_queries(b, g):
-            planes = q_stage.tile([P, PACK, S], BF16, name="q_planes")
+        def flip_tokens(b, g, u):
+            grouped_words = x_grouped[b][:].bitcast(F32)
+            words = x_raw[(b, g)][:].bitcast(F32).rearrange("p u (a q w) -> p u a w q", a=PASSES, w=2)
+            flipped = psum.tile([P, PASSES, 2, P], F32, tag="bank", name="flipped")
+            for kp in range(PASSES):
+                for w in range(2):
+                    nc.tensor.transpose(flipped[:, kp, w, :], words[:, u, kp, w, :], identity[:])
+            first = (2 * g + u) * P
+            nc.scalar.copy(
+                out=grouped_words[:, :, first : first + P, :],
+                in_=flipped[:].rearrange("p a w c -> p a c w"),
+            )
+
+        def quantise_tokens(b, g):
+            tokens = slice(2 * P * g, 2 * P * (g + 1))
+            for kp in range(PASSES):
+                quantise(x_mx[b], kp, tokens, x_grouped[b][:, kp, tokens, :])
+
+        w_mx = {"q": mx_operand("wq", D), "v": mx_operand("wv", D)}
+        column_order = {"q": "p (i c) t -> p c t i", "v": "p (c i) t -> p c t i"}
+        w_grouped_tiles = {}
+
+        def regroup_weight(label, half, kp, vector_runs):
+            w_grouped = keep.tile([P, BANK, PACK], BF16, name="w_grouped_%s_%d_%d" % (label, half, kp), align_bytes=64)
+            source = w_raw[(label, half, kp)][:].rearrange("p t (c i) -> p c t i", i=RUN)
+            target = w_grouped[:].rearrange(column_order[label], i=RUN)
+            if vector_runs > 0:
+                nc.vector.tensor_copy(out=target[:, 0:vector_runs], in_=source[:, 0:vector_runs])
+            if vector_runs < RUNS:
+                nc.scalar.copy(out=target[:, vector_runs:RUNS], in_=source[:, vector_runs:RUNS])
+            w_grouped_tiles[(label, half, kp)] = w_grouped
+
+        def quantise_weight(label, half, kp):
+            quantise(w_mx[label], kp, slice(BANK * half, BANK * (half + 1)), w_grouped_tiles[(label, half, kp)][:])
+
+        bv_words = keep.tile([P, 4, P], F32, name="bv_words")
+
+        def spread_bv():
+            pairs = bv_pairs[:].rearrange("p c e -> p (c e)").bitcast(F32)
+            spread = psum.tile([P, 4, P], F32, tag="bank", name="spread")
+            for c in range(4):
+                nc.tensor.transpose(spread[:, c, :], pairs[:, c : c + 1].to_broadcast([P, P]), identity[:])
+            nc.scalar.copy(out=bv_words[:], in_=spread[:])
+
+        v_mx = [mx_operand("v%d" % b, S) for b in range(B)]
+        q_mx = [mx_operand("q%d" % b, S) for b in range(B)]
+        q_grouped = {}
+        v_rows = {}
+        v_grouped = {}
+        for b in range(B):
+            for g in range(PASSES):
+                q_grouped[(b, g)] = keep.tile([P, S, PACK], BF16, name="q_grouped_%d_%d" % (b, g), align_bytes=64)
+                v_grouped[(b, g)] = keep.tile([P, BANK, PACK], BF16, name="v_grouped_%d_%d" % (b, g), align_bytes=64)
+                v_rows[(b, g)] = keep.tile([P, 2, D], F32, name="v_rows_%d_%d" % (b, g))
+
+        q_banks = {}
+
+        def multiply_queries(b, g, i):
+            tokens = slice(P * i, P * (i + 1))
+            acc = psum.tile([P, PACK, P], F32, tag="bank", name="q_bank")
             for t in range(PACK):
                 features = slice(K_PASS * g + P * t, K_PASS * g + P * (t + 1))
-                acc = psum.tile([P, BANK], F32, tag="bank")
                 for kp in range(PASSES):
-                    mx_pass(acc[:], kp, w_mx["q"], features, x_mx[b], slice(0, S))
-                nc.scalar.activation(
-                    out=planes[:, t, :], in_=acc[:], func=mybir.ActivationFunctionType.Identity,
-                    bias=bq_column[:, PACK * g + t : PACK * g + t + 1], scale=1.0,
-                )
-            q_planes[(b, g)] = planes
+                    mx_pass(acc[:, t, :], kp, w_mx["q"], features, x_mx[b], tokens)
+            q_banks[(b, g, i)] = acc
+
+        def group_queries(b, g, i):
+            tokens = slice(P * i, P * (i + 1))
+            nc.vector.tensor_tensor(
+                out=q_grouped[(b, g)][:, tokens, :],
+                in0=q_banks[(b, g, i)][:].rearrange("p t n -> p n t"),
+                in1=bq_cols[:, g, :].unsqueeze(1).to_broadcast([P, P, PACK]),
+                op=ADD,
+            )
+
+        q_planes = {}
+
+        def project_query_plane(b, g, t):
+            acc = psum.tile([P, BANK], F32, tag="bank", name="q_plane_bank")
+            features = slice(K_PASS * g + P * t, K_PASS * g + P * (t + 1))
+            for kp in range(PASSES):
+                mx_pass(acc[:], kp, w_mx["q"], features, x_mx[b], slice(0, S))
+            if t == 0:
+                q_planes[(b, g)] = keep.tile([P, PACK, S], BF16, name="q_planes_%d_%d" % (b, g))
+            nc.scalar.activation(
+                out=q_planes[(b, g)][:, t, :], in_=acc[:], func=mybir.ActivationFunctionType.Identity,
+                bias=bq_cols[:, g, t : t + 1], scale=1.0,
+            )
 
         def regroup_queries(b, g):
-            q_grouped = q_stage.tile([P, S, PACK], BF16, align_bytes=64)
             nc.vector.tensor_copy(
-                out=q_grouped[:].rearrange("p (c i) t -> p c t i", i=RUN),
+                out=q_grouped[(b, g)][:].rearrange("p (c i) t -> p c t i", i=RUN),
                 in_=q_planes[(b, g)][:].rearrange("p t (c i) -> p c t i", i=RUN),
             )
-            grouped_tiles[("q", b, g)] = q_grouped
 
-        def quantise_queries(b, g):
-            quantise(q_mx[b], g, slice(0, S), grouped_tiles[("q", b, g)][:])
+        def quantise_queries(b, g, first, last):
+            tokens = slice(P * first, P * last)
+            quantise(q_mx[b], g, tokens, q_grouped[(b, g)][:, tokens, :])
 
-        def project_values(b, g):
-            rows = results.tile([P, 2, D], F32, name="v_rows")
+        v_banks = {}
+
+        def multiply_values(b, g, h):
+            columns = slice(BANK * h, BANK * (h + 1))
             for u in range(2):
                 tokens = slice((2 * g + u) * P, (2 * g + u + 1) * P)
-                for h in range(HALVES):
-                    columns = slice(BANK * h, BANK * (h + 1))
-                    acc = psum.tile([P, BANK], F32, tag="bank")
-                    for kp in range(PASSES):
-                        mx_pass(acc[:], kp, x_mx[b], tokens, w_mx["v"], columns)
-                    nc.vector.tensor_tensor(
-                        out=rows[:, u, columns], in0=acc[:], in1=bv_all[:, h, :], op=mybir.AluOpType.add
-                    )
+                acc = psum.tile([P, BANK], F32, tag="bank", name="v_bank")
+                for kp in range(PASSES):
+                    mx_pass(acc[:], kp, x_mx[b], tokens, w_mx["v"], columns)
+                v_banks[(b, g, h, u)] = acc
+
+        def add_bv(b, g, h):
+            columns = slice(BANK * h, BANK * (h + 1))
+            for u in range(2):
+                nc.vector.tensor_tensor(
+                    out=v_rows[(b, g)][:, u, columns],
+                    in0=v_banks[(b, g, h, u)][:],
+                    in1=bv_words[:].rearrange("p c n -> p (c n)").bitcast(BF16)[:, columns],
+                    op=ADD,
+                )
+
+        def store_values(b, g):
             nc.sync.dma_start(
                 out=out_1[b, 2 * P * g : 2 * P * (g + 1), :].rearrange("(p u) n -> p (u n)", u=2),
-                in_=rows[:].rearrange("p u n -> p (u n)"),
+                in_=v_rows[(b, g)][:].rearrange("p u n -> p (u n)"),
             )
-            v_rows[(b, g)] = rows
 
-        def regroup_values(b, g):
-            v_grouped = v_stage.tile([P, BANK, PACK], BF16, align_bytes=64)
-            nc.scalar.copy(
-                out=v_grouped[:].rearrange("p (c i) t -> p c t i", i=RUN),
-                in_=v_rows[(b, g)][:].rearrange("p u (h c i) -> p c (u h) i", h=HALVES, i=RUN),
-            )
-            grouped_tiles[("v", b, g)] = v_grouped
+        def regroup_values_scalar(b, g, columns):
+            source = v_rows[(b, g)][:].rearrange("p u (h c i) -> p c (u h) i", h=HALVES, i=RUN)
+            target = v_grouped[(b, g)][:].rearrange("p (c i) t -> p c t i", i=RUN)
+            runs = slice(columns.start // RUN, columns.stop // RUN)
+            nc.scalar.copy(out=target[:, runs], in_=source[:, runs])
+
+        def regroup_values(b, g, parts=(0, 1)):
+            source = v_rows[(b, g)][:].rearrange("p u (h c) -> p c (u h)", h=HALVES)
+            for part in parts:
+                columns = slice(256 * part, 256 * (part + 1))
+                nc.gpsimd.tensor_scalar(
+                    out=v_grouped[(b, g)][:, columns, :], in0=source[:, columns, :],
+                    scalar1=1.0, scalar2=0.0, op0=MULT, op1=ADD,
+                )
 
         def quantise_values(b, g):
-            quantise(v_mx[b], g, slice(0, S), grouped_tiles[("v", b, g)][:])
+            quantise(v_mx[b], g, slice(0, S), v_grouped[(b, g)][:])
 
-        def add_scores(b, g):
-            if g == 0:
-                score_banks[b] = [psum.tile([P, BANK], F32, tag="bank", name="score_bank") for i in range(S // P)]
-            for i in range(S // P):
-                mx_pass(score_banks[b][i][:], g, q_mx[b], slice(P * i, P * (i + 1)), v_mx[b], slice(0, S))
+        score_banks = {}
 
-        def store_scores(b):
+        def multiply_scores(b, i):
+            acc = psum.tile([P, BANK], F32, tag="bank", name="score_bank")
             for g in range(PASSES):
-                score_rows = results.tile([P, 2, S], F32)
-                nc.scalar.mul(out=score_rows[:, 0, :], in_=score_banks[b][2 * g][:], mul=1.0 / math.sqrt(D))
-                nc.vector.tensor_scalar_mul(
-                    out=score_rows[:, 1, :], in0=score_banks[b][2 * g + 1][:], scalar1=1.0 / math.sqrt(D)
-                )
-                rows_out = out_0[b, 2 * P * g : 2 * P * (g + 1), :].rearrange("(p u) j -> p u j", u=2)
-                for u in range(2):
-                    nc.sync.dma_start(out=rows_out[:, u, :], in_=score_rows[:, u, :])
+                mx_pass(acc[:], g, q_mx[b], slice(P * i, P * (i + 1)), v_mx[b], slice(0, S))
+            score_banks[(b, i)] = acc
 
-        regroup_weight_half("q", 0)
-        quantise_weight_half("q", 0)
-        spread_biases()
-        flip_tokens(0)
-        quantise_tokens(0)
-        regroup_weight_half("q", 1)
-        quantise_weight_half("q", 1)
-        project_queries(0, 0)
-        project_queries(0, 1)
-        regroup_weight_half("v", 0)
-        regroup_queries(0, 0)
-        regroup_weight_half("v", 1)
-        quantise_queries(0, 0)
-        regroup_queries(0, 1)
-        quantise_weight_half("v", 0)
-        quantise_queries(0, 1)
-        quantise_weight_half("v", 1)
-        flip_tokens(1)
-        project_values(0, 0)
-        quantise_tokens(1)
-        project_values(0, 1)
+        def store_scores(b, i):
+            rows = keep.tile([P, S], F32, name="score_rows_%d_%d" % (b, i))
+            nc.scalar.mul(out=rows[:], in_=score_banks[(b, i)][:], mul=1.0 / math.sqrt(D))
+            g, u = divmod(i, 2)
+            rows_out = out_0[b, 2 * P * g : 2 * P * (g + 1), :].rearrange("(p u) j -> p u j", u=2)
+            nc.sync.dma_start(out=rows_out[:, u, :], in_=rows[:])
+
+        regroup_weight("v", 0, 0, 84)
+        flip_tokens(0, 0, 0)
+        flip_tokens(0, 0, 1)
+        quantise_weight("v", 0, 0)
+        regroup_weight("v", 0, 1, 100)
+        quantise_tokens(0, 0)
+        quantise_weight("v", 0, 1)
+        flip_tokens(0, 1, 0)
+        flip_tokens(0, 1, 1)
+        spread_bv()
+        multiply_values(0, 0, 0)
+        regroup_weight("v", 1, 0, 72)
+        quantise_tokens(0, 1)
+        add_bv(0, 0, 0)
+        multiply_values(0, 1, 0)
+        regroup_weight("v", 1, 1, 64)
+        add_bv(0, 1, 0)
+        quantise_weight("v", 1, 0)
+        quantise_weight("v", 1, 1)
+        for g in range(PASSES):
+            for u in range(2):
+                flip_tokens(1, g, u)
+        multiply_values(0, 0, 1)
+        multiply_values(0, 1, 1)
+        regroup_weight("q", 0, 0, 32)
+        add_bv(0, 0, 1)
+        store_values(0, 0)
         regroup_values(0, 0)
-        quantise_values(0, 0)
-        project_queries(1, 0)
-        project_values(1, 0)
+        add_bv(0, 1, 1)
+        store_values(0, 1)
+        quantise_tokens(1, 0)
+        quantise_tokens(1, 1)
+        regroup_weight("q", 0, 1, 32)
+        multiply_values(1, 0, 0)
+        multiply_values(1, 0, 1)
+        quantise_weight("q", 0, 0)
+        add_bv(1, 0, 0)
+        add_bv(1, 0, 1)
+        store_values(1, 0)
         regroup_values(0, 1)
-        regroup_queries(1, 0)
-        quantise_values(0, 1)
-        quantise_queries(1, 0)
-        add_scores(0, 0)
-        project_queries(1, 1)
-        add_scores(0, 1)
-        store_scores(0)
-        project_values(1, 1)
+        regroup_weight("q", 1, 0, 24)
+        quantise_weight("q", 0, 1)
+        regroup_weight("q", 1, 1, 24)
+        multiply_values(1, 1, 0)
+        multiply_values(1, 1, 1)
+        add_bv(1, 1, 0)
+        add_bv(1, 1, 1)
+        store_values(1, 1)
+        for t in range(PACK):
+            project_query_plane(0, 0, t)
         regroup_values(1, 0)
-        regroup_queries(1, 1)
+        quantise_weight("q", 1, 0)
+        regroup_values_scalar(1, 1, slice(0, 256))
+        regroup_values(1, 1, (1,))
+        quantise_values(0, 0)
+        quantise_weight("q", 1, 1)
+        for t in range(PACK):
+            project_query_plane(0, 1, t)
+        for i in range(GROUPS):
+            multiply_queries(1, 0, i)
+        regroup_queries(0, 0)
+        quantise_values(0, 1)
+        quantise_queries(0, 0, 0, 4)
+        group_queries(1, 0, 0)
+        group_queries(1, 0, 1)
+        regroup_queries(0, 1)
+        group_queries(1, 0, 2)
+        group_queries(1, 0, 3)
+        quantise_queries(0, 1, 0, 4)
+        multiply_queries(1, 1, 0)
+        multiply_queries(1, 1, 1)
+        multiply_scores(0, 0)
+        multiply_scores(0, 1)
+        multiply_queries(1, 1, 2)
+        multiply_queries(1, 1, 3)
+        multiply_scores(0, 2)
+        multiply_scores(0, 3)
+        for i in range(GROUPS):
+            store_scores(0, i)
         quantise_values(1, 0)
-        quantise_queries(1, 1)
-        add_scores(1, 0)
-        regroup_values(1, 1)
+        group_queries(1, 1, 0)
         quantise_values(1, 1)
-        add_scores(1, 1)
-        store_scores(1)
+        quantise_queries(1, 0, 0, 4)
+        group_queries(1, 1, 1)
+        quantise_queries(1, 1, 0, 1)
+        group_queries(1, 1, 2)
+        quantise_queries(1, 1, 1, 2)
+        group_queries(1, 1, 3)
+        quantise_queries(1, 1, 2, 3)
+        quantise_queries(1, 1, 3, 4)
+        for i in range(GROUPS):
+            multiply_scores(1, i)
+            store_scores(1, i)

@@ -10,7 +10,6 @@ U32 = mybir.dt.uint32
 U8 = mybir.dt.uint8
 FP8X4 = mybir.dt.float8_e4m3fn_x4
 ADD = mybir.AluOpType.add
-MULT = mybir.AluOpType.mult
 
 P = 128
 PACK = 4
@@ -229,20 +228,10 @@ def tile_selfattention_pa_kernel(tc, X, Wq, bq, Wv, bv, out_0, out_1):
                 in_=v_rows[(b, g)][:].rearrange("p u n -> p (u n)"),
             )
 
-        def regroup_values_scalar(b, g, columns):
+        def regroup_values(b, g):
             source = v_rows[(b, g)][:].rearrange("p u (h c i) -> p c (u h) i", h=HALVES, i=RUN)
             target = v_grouped[(b, g)][:].rearrange("p (c i) t -> p c t i", i=RUN)
-            runs = slice(columns.start // RUN, columns.stop // RUN)
-            nc.scalar.copy(out=target[:, runs], in_=source[:, runs])
-
-        def regroup_values(b, g, parts=(0, 1)):
-            source = v_rows[(b, g)][:].rearrange("p u (h c) -> p c (u h)", h=HALVES)
-            for part in parts:
-                columns = slice(256 * part, 256 * (part + 1))
-                nc.gpsimd.tensor_scalar(
-                    out=v_grouped[(b, g)][:, columns, :], in0=source[:, columns, :],
-                    scalar1=1.0, scalar2=0.0, op0=MULT, op1=ADD,
-                )
+            nc.scalar.copy(out=target, in_=source)
 
         def quantise_values(b, g):
             quantise(v_mx[b], g, slice(0, S), v_grouped[(b, g)][:])
@@ -255,9 +244,12 @@ def tile_selfattention_pa_kernel(tc, X, Wq, bq, Wv, bv, out_0, out_1):
                 mx_pass(acc[:], g, q_mx[b], slice(P * i, P * (i + 1)), v_mx[b], slice(0, S))
             score_banks[(b, i)] = acc
 
-        def store_scores(b, i):
+        def store_scores(b, i, engine):
             rows = keep.tile([P, S], F32, name="score_rows_%d_%d" % (b, i))
-            nc.scalar.mul(out=rows[:], in_=score_banks[(b, i)][:], mul=1.0 / math.sqrt(D))
+            if engine == "scalar":
+                nc.scalar.mul(out=rows[:], in_=score_banks[(b, i)][:], mul=1.0 / math.sqrt(D))
+            else:
+                nc.vector.tensor_scalar_mul(out=rows[:], in0=score_banks[(b, i)][:], scalar1=1.0 / math.sqrt(D))
             g, u = divmod(i, 2)
             rows_out = out_0[b, 2 * P * g : 2 * P * (g + 1), :].rearrange("(p u) j -> p u j", u=2)
             nc.sync.dma_start(out=rows_out[:, u, :], in_=rows[:])
@@ -286,66 +278,63 @@ def tile_selfattention_pa_kernel(tc, X, Wq, bq, Wv, bv, out_0, out_1):
                 flip_tokens(1, g, u)
         multiply_values(0, 0, 1)
         multiply_values(0, 1, 1)
-        regroup_weight("q", 0, 0, 32)
+        regroup_weight("q", 0, 0, 40)
         add_bv(0, 0, 1)
         store_values(0, 0)
-        regroup_values(0, 0)
         add_bv(0, 1, 1)
         store_values(0, 1)
         quantise_tokens(1, 0)
         quantise_tokens(1, 1)
-        regroup_weight("q", 0, 1, 32)
+        regroup_weight("q", 0, 1, 40)
         multiply_values(1, 0, 0)
         multiply_values(1, 0, 1)
         quantise_weight("q", 0, 0)
         add_bv(1, 0, 0)
         add_bv(1, 0, 1)
         store_values(1, 0)
-        regroup_values(0, 1)
-        regroup_weight("q", 1, 0, 24)
+        regroup_weight("q", 1, 0, 32)
         quantise_weight("q", 0, 1)
-        regroup_weight("q", 1, 1, 24)
+        regroup_weight("q", 1, 1, 32)
         multiply_values(1, 1, 0)
         multiply_values(1, 1, 1)
+        regroup_values(0, 0)
+        for t in range(PACK):
+            project_query_plane(0, 0, t)
+        regroup_values(0, 1)
         add_bv(1, 1, 0)
         add_bv(1, 1, 1)
         store_values(1, 1)
-        for t in range(PACK):
-            project_query_plane(0, 0, t)
-        regroup_values(1, 0)
         quantise_weight("q", 1, 0)
-        regroup_values_scalar(1, 1, slice(0, 256))
-        regroup_values(1, 1, (1,))
         quantise_values(0, 0)
         quantise_weight("q", 1, 1)
-        for t in range(PACK):
-            project_query_plane(0, 1, t)
         for i in range(GROUPS):
             multiply_queries(1, 0, i)
+        for t in range(PACK):
+            project_query_plane(0, 1, t)
+        regroup_values(1, 0)
         regroup_queries(0, 0)
-        quantise_values(0, 1)
-        quantise_queries(0, 0, 0, 4)
         group_queries(1, 0, 0)
         group_queries(1, 0, 1)
-        regroup_queries(0, 1)
+        quantise_queries(0, 0, 0, 4)
+        quantise_values(0, 1)
         group_queries(1, 0, 2)
         group_queries(1, 0, 3)
+        regroup_queries(0, 1)
+        quantise_queries(1, 0, 0, 4)
         quantise_queries(0, 1, 0, 4)
         multiply_queries(1, 1, 0)
         multiply_queries(1, 1, 1)
-        multiply_scores(0, 0)
-        multiply_scores(0, 1)
+        for i in range(GROUPS):
+            multiply_scores(0, i)
         multiply_queries(1, 1, 2)
         multiply_queries(1, 1, 3)
-        multiply_scores(0, 2)
-        multiply_scores(0, 3)
+        regroup_values(1, 1)
         for i in range(GROUPS):
-            store_scores(0, i)
+            store_scores(0, i, "scalar")
         quantise_values(1, 0)
         group_queries(1, 1, 0)
-        quantise_values(1, 1)
-        quantise_queries(1, 0, 0, 4)
         group_queries(1, 1, 1)
+        quantise_values(1, 1)
         quantise_queries(1, 1, 0, 1)
         group_queries(1, 1, 2)
         quantise_queries(1, 1, 1, 2)
@@ -354,4 +343,4 @@ def tile_selfattention_pa_kernel(tc, X, Wq, bq, Wv, bv, out_0, out_1):
         quantise_queries(1, 1, 3, 4)
         for i in range(GROUPS):
             multiply_scores(1, i)
-            store_scores(1, i)
+            store_scores(1, i, "scalar" if i % 2 == 0 else "vector")

@@ -32,9 +32,7 @@ def tile_selfattention_pa_kernel(tc, X, Wq, bq, Wv, bv, out_0, out_1):
         psum = ctx.enter_context(tc.psum_pool(name="psum", bufs=8))
         ctx.enter_context(tc.manual_schedule())
         bq_cols = keep.tile([P, PASSES, PACK], BF16, name="bq_cols")
-        nc.scalar.dma_start(out=bq_cols[:], in_=bq.rearrange("(g p t) -> p g t", g=PASSES, t=PACK))
         bv_pairs = keep.tile([P, 4, 2], BF16, name="bv_pairs")
-        nc.scalar.dma_start(out=bv_pairs[:], in_=bv.rearrange("(c p e) -> p c e", c=4, e=2))
         identity = keep.tile([P, P], F32, name="identity")
         make_identity(nc, identity[:])
 
@@ -64,12 +62,14 @@ def tile_selfattention_pa_kernel(tc, X, Wq, bq, Wv, bv, out_0, out_1):
         load_tokens(0, 0)
         load_weight("v", 0, 1)
         load_tokens(0, 1)
+        nc.sync.dma_start(out=bv_pairs[:], in_=bv.rearrange("(c p e) -> p c e", c=4, e=2))
         load_weight("v", 1, 0)
         load_weight("v", 1, 1)
         load_tokens(1, 0)
         load_tokens(1, 1)
         load_weight("q", 0, 0)
         load_weight("q", 0, 1)
+        nc.sync.dma_start(out=bq_cols[:], in_=bq.rearrange("(g p t) -> p g t", g=PASSES, t=PACK))
         load_weight("q", 1, 0)
         load_weight("q", 1, 1)
 
@@ -238,11 +238,10 @@ def tile_selfattention_pa_kernel(tc, X, Wq, bq, Wv, bv, out_0, out_1):
 
         score_banks = {}
 
-        def multiply_scores(b, i):
-            acc = psum.tile([P, BANK], F32, tag="bank", name="score_bank")
-            for g in range(PASSES):
-                mx_pass(acc[:], g, q_mx[b], slice(P * i, P * (i + 1)), v_mx[b], slice(0, S))
-            score_banks[(b, i)] = acc
+        def score_pass(b, i, g):
+            if g == 0:
+                score_banks[(b, i)] = psum.tile([P, BANK], F32, tag="bank", name="score_bank")
+            mx_pass(score_banks[(b, i)][:], g, q_mx[b], slice(P * i, P * (i + 1)), v_mx[b], slice(0, S))
 
         def store_scores(b, i, engine):
             rows = keep.tile([P, S], F32, name="score_rows_%d_%d" % (b, i))
@@ -322,12 +321,11 @@ def tile_selfattention_pa_kernel(tc, X, Wq, bq, Wv, bv, out_0, out_1):
         regroup_queries(0, 1)
         quantise_queries(1, 0, 0, 4)
         quantise_queries(0, 1, 0, 4)
-        multiply_queries(1, 1, 0)
-        multiply_queries(1, 1, 1)
         for i in range(GROUPS):
-            multiply_scores(0, i)
-        multiply_queries(1, 1, 2)
-        multiply_queries(1, 1, 3)
+            multiply_queries(1, 1, i)
+        for i in range(GROUPS):
+            for g in range(PASSES):
+                score_pass(0, i, g)
         regroup_values(1, 1)
         for i in range(GROUPS):
             store_scores(0, i, "scalar")
@@ -335,12 +333,21 @@ def tile_selfattention_pa_kernel(tc, X, Wq, bq, Wv, bv, out_0, out_1):
         group_queries(1, 1, 0)
         group_queries(1, 1, 1)
         quantise_values(1, 1)
+        score_pass(1, 0, 0)
+        score_pass(1, 1, 0)
         quantise_queries(1, 1, 0, 1)
+        score_pass(1, 0, 1)
+        store_scores(1, 0, "scalar")
         group_queries(1, 1, 2)
+        score_pass(1, 2, 0)
         quantise_queries(1, 1, 1, 2)
+        score_pass(1, 1, 1)
+        store_scores(1, 1, "scalar")
         group_queries(1, 1, 3)
+        score_pass(1, 3, 0)
         quantise_queries(1, 1, 2, 3)
+        score_pass(1, 2, 1)
         quantise_queries(1, 1, 3, 4)
-        for i in range(GROUPS):
-            multiply_scores(1, i)
-            store_scores(1, i, "scalar" if i % 2 == 0 else "vector")
+        score_pass(1, 3, 1)
+        store_scores(1, 2, "vector")
+        store_scores(1, 3, "scalar")

import math
from contextlib import ExitStack

import concourse.mybir as mybir
from concourse.masks import make_identity

F32 = mybir.dt.float32
BF16 = mybir.dt.bfloat16
U32 = mybir.dt.uint32
U8 = mybir.dt.uint8
FP8X4 = mybir.dt.float8_e4m3fn_x4
ADD = mybir.AluOpType.add

P = 128
PACK = 4
K_PASS = P * PACK
B, S, D = 2, 512, 1024
PASSES = D // K_PASS
BANK = 512
HALVES = D // BANK
GROUPS = S // P
RUN = 4
RUNS = BANK // RUN

FLOPS = 2 * (2 * B * S * D * D) + 2 * B * S * S * D


def tile_selfattention_pa_kernel(tc, X, Wq, bq, Wv, bv, out_0, out_1):
    nc = tc.nc
    with ExitStack() as ctx:
        keep = ctx.enter_context(tc.tile_pool(name="keep", bufs=1))
        psum = ctx.enter_context(tc.psum_pool(name="psum", bufs=8))
        ctx.enter_context(tc.manual_schedule())
        bq_cols = keep.tile([P, PASSES, PACK], BF16, name="bq_cols")
        bv_pairs = keep.tile([P, 4, 2], BF16, name="bv_pairs")
        identity = keep.tile([P, P], F32, name="identity")
        make_identity(nc, identity[:])

        x_raw = {}
        w_raw = {}

        def load_tokens(b, g):
            rows = keep.tile([P, 2, D], BF16, name="x_raw_%d_%d" % (b, g))
            nc.sync.dma_start(
                out=rows[:].rearrange("p u k -> p (u k)"),
                in_=X[b, 2 * P * g : 2 * P * (g + 1), :].rearrange("(p u) k -> p (u k)", u=2),
            )
            x_raw[(b, g)] = rows

        def load_weight(label, half, kp):
            W = Wq if label == "q" else Wv
            rows = keep.tile([P, PACK, BANK], BF16, name="w_raw_%s_%d_%d" % (label, half, kp))
            nc.sync.dma_start(
                out=rows[:],
                in_=W[K_PASS * kp : K_PASS * (kp + 1), BANK * half : BANK * (half + 1)].rearrange(
                    "(p t) n -> p t n", t=PACK
                ),
            )
            w_raw[(label, half, kp)] = rows

        load_weight("v", 0, 0)
        load_tokens(0, 0)
        load_weight("v", 0, 1)
        load_tokens(0, 1)
        nc.sync.dma_start(out=bv_pairs[:], in_=bv.rearrange("(c p e) -> p c e", c=4, e=2))
        load_weight("v", 1, 0)
        load_weight("v", 1, 1)
        load_tokens(1, 0)
        load_tokens(1, 1)
        load_weight("q", 0, 0)
        load_weight("q", 0, 1)
        nc.sync.dma_start(out=bq_cols[:], in_=bq.rearrange("(g p t) -> p g t", g=PASSES, t=PACK))
        load_weight("q", 1, 0)
        load_weight("q", 1, 1)

        def mx_operand(label, columns):
            codes = keep.tile([P, PASSES, columns], U32, name="%s_codes" % label, align_bytes=64)
            scales = keep.tile([P, PASSES, columns], U8, name="%s_scales" % label, align_bytes=64)
            return codes, scales

        def quantise(operand, kp, columns, grouped):
            codes, scales = operand
            nc.vector.quantize_mx(
                out=codes[:, kp, columns].bitcast(FP8X4),
                scales=scales[:, kp, columns],
                in_=grouped.rearrange("p c t -> p (c t)"),
            )

        def mx_pass(acc, kp, stationary, stationary_columns, moving, moving_columns):
            nc.tensor.matmul_mx(
                out=acc,
                lhsT=stationary[0][:, kp, stationary_columns].bitcast(FP8X4),
                lhsT_scale=stationary[1][:, kp, stationary_columns],
                rhs=moving[0][:, kp, moving_columns].bitcast(FP8X4),
                rhs_scale=moving[1][:, kp, moving_columns],
                start=(kp == 0),
                stop=(kp == PASSES - 1),
            )

        x_mx = [mx_operand("x%d" % b, S) for b in range(B)]
        x_grouped = [
            keep.tile([P, PASSES, S, PACK], BF16, name="x_grouped_%d" % b, align_bytes=64) for b in range(B)
        ]

        def flip_tokens(b, g, u):
            grouped_words = x_grouped[b][:].bitcast(F32)
            words = x_raw[(b, g)][:].bitcast(F32).rearrange("p u (a q w) -> p u a w q", a=PASSES, w=2)
            flipped = psum.tile([P, PASSES, 2, P], F32, tag="bank", name="flipped")
            for kp in range(PASSES):
                for w in range(2):
                    nc.tensor.transpose(flipped[:, kp, w, :], words[:, u, kp, w, :], identity[:])
            first = (2 * g + u) * P
            nc.scalar.copy(
                out=grouped_words[:, :, first : first + P, :],
                in_=flipped[:].rearrange("p a w c -> p a c w"),
            )

        def quantise_tokens(b, g):
            tokens = slice(2 * P * g, 2 * P * (g + 1))
            for kp in range(PASSES):
                quantise(x_mx[b], kp, tokens, x_grouped[b][:, kp, tokens, :])

        w_mx = {"q": mx_operand("wq", D), "v": mx_operand("wv", D)}
        column_order = {"q": "p (i c) t -> p c t i", "v": "p (c i) t -> p c t i"}
        w_grouped_tiles = {}

        def regroup_weight(label, half, kp, vector_runs):
            w_grouped = keep.tile([P, BANK, PACK], BF16, name="w_grouped_%s_%d_%d" % (label, half, kp), align_bytes=64)
            source = w_raw[(label, half, kp)][:].rearrange("p t (c i) -> p c t i", i=RUN)
            target = w_grouped[:].rearrange(column_order[label], i=RUN)
            if vector_runs > 0:
                nc.vector.tensor_copy(out=target[:, 0:vector_runs], in_=source[:, 0:vector_runs])
            if vector_runs < RUNS:
                nc.scalar.copy(out=target[:, vector_runs:RUNS], in_=source[:, vector_runs:RUNS])
            w_grouped_tiles[(label, half, kp)] = w_grouped

        def quantise_weight(label, half, kp):
            quantise(w_mx[label], kp, slice(BANK * half, BANK * (half + 1)), w_grouped_tiles[(label, half, kp)][:])

        bv_words = keep.tile([P, 4, P], F32, name="bv_words")

        def spread_bv():
            pairs = bv_pairs[:].rearrange("p c e -> p (c e)").bitcast(F32)
            spread = psum.tile([P, 4, P], F32, tag="bank", name="spread")
            for c in range(4):
                nc.tensor.transpose(spread[:, c, :], pairs[:, c : c + 1].to_broadcast([P, P]), identity[:])
            nc.scalar.copy(out=bv_words[:], in_=spread[:])

        v_mx = [mx_operand("v%d" % b, S) for b in range(B)]
        q_mx = [mx_operand("q%d" % b, S) for b in range(B)]
        q_grouped = {}
        v_rows = {}
        v_grouped = {}
        for b in range(B):
            for g in range(PASSES):
                q_grouped[(b, g)] = keep.tile([P, S, PACK], BF16, name="q_grouped_%d_%d" % (b, g), align_bytes=64)
                v_grouped[(b, g)] = keep.tile([P, BANK, PACK], BF16, name="v_grouped_%d_%d" % (b, g), align_bytes=64)
                v_rows[(b, g)] = keep.tile([P, 2, D], F32, name="v_rows_%d_%d" % (b, g))

        q_banks = {}

        def multiply_queries(b, g, i):
            tokens = slice(P * i, P * (i + 1))
            acc = psum.tile([P, PACK, P], F32, tag="bank", name="q_bank")
            for t in range(PACK):
                features = slice(K_PASS * g + P * t, K_PASS * g + P * (t + 1))
                for kp in range(PASSES):
                    mx_pass(acc[:, t, :], kp, w_mx["q"], features, x_mx[b], tokens)
            q_banks[(b, g, i)] = acc

        def group_queries(b, g, i):
            tokens = slice(P * i, P * (i + 1))
            nc.vector.tensor_tensor(
                out=q_grouped[(b, g)][:, tokens, :],
                in0=q_banks[(b, g, i)][:].rearrange("p t n -> p n t"),
                in1=bq_cols[:, g, :].unsqueeze(1).to_broadcast([P, P, PACK]),
                op=ADD,
            )

        q_planes = {}

        def project_query_plane(b, g, t):
            acc = psum.tile([P, BANK], F32, tag="bank", name="q_plane_bank")
            features = slice(K_PASS * g + P * t, K_PASS * g + P * (t + 1))
            for kp in range(PASSES):
                mx_pass(acc[:], kp, w_mx["q"], features, x_mx[b], slice(0, S))
            if t == 0:
                q_planes[(b, g)] = keep.tile([P, PACK, S], BF16, name="q_planes_%d_%d" % (b, g))
            nc.scalar.activation(
                out=q_planes[(b, g)][:, t, :], in_=acc[:], func=mybir.ActivationFunctionType.Identity,
                bias=bq_cols[:, g, t : t + 1], scale=1.0,
            )

        def regroup_queries(b, g):
            nc.vector.tensor_copy(
                out=q_grouped[(b, g)][:].rearrange("p (c i) t -> p c t i", i=RUN),
                in_=q_planes[(b, g)][:].rearrange("p t (c i) -> p c t i", i=RUN),
            )

        def quantise_queries(b, g, first, last):
            tokens = slice(P * first, P * last)
            quantise(q_mx[b], g, tokens, q_grouped[(b, g)][:, tokens, :])

        v_banks = {}

        def multiply_values(b, g, h):
            columns = slice(BANK * h, BANK * (h + 1))
            for u in range(2):
                tokens = slice((2 * g + u) * P, (2 * g + u + 1) * P)
                acc = psum.tile([P, BANK], F32, tag="bank", name="v_bank")
                for kp in range(PASSES):
                    mx_pass(acc[:], kp, x_mx[b], tokens, w_mx["v"], columns)
                v_banks[(b, g, h, u)] = acc

        def add_bv(b, g, h):
            columns = slice(BANK * h, BANK * (h + 1))
            for u in range(2):
                nc.vector.tensor_tensor(
                    out=v_rows[(b, g)][:, u, columns],
                    in0=v_banks[(b, g, h, u)][:],
                    in1=bv_words[:].rearrange("p c n -> p (c n)").bitcast(BF16)[:, columns],
                    op=ADD,
                )

        def store_values(b, g):
            nc.sync.dma_start(
                out=out_1[b, 2 * P * g : 2 * P * (g + 1), :].rearrange("(p u) n -> p (u n)", u=2),
                in_=v_rows[(b, g)][:].rearrange("p u n -> p (u n)"),
            )

        def regroup_values(b, g):
            source = v_rows[(b, g)][:].rearrange("p u (h c i) -> p c (u h) i", h=HALVES, i=RUN)
            target = v_grouped[(b, g)][:].rearrange("p (c i) t -> p c t i", i=RUN)
            nc.scalar.copy(out=target, in_=source)

        def quantise_values(b, g):
            quantise(v_mx[b], g, slice(0, S), v_grouped[(b, g)][:])

        score_banks = {}

        def score_pass(b, i, g):
            if g == 0:
                score_banks[(b, i)] = psum.tile([P, BANK], F32, tag="bank", name="score_bank")
            mx_pass(score_banks[(b, i)][:], g, q_mx[b], slice(P * i, P * (i + 1)), v_mx[b], slice(0, S))

        def store_scores(b, i, engine):
            rows = keep.tile([P, S], F32, name="score_rows_%d_%d" % (b, i))
            if engine == "scalar":
                nc.scalar.mul(out=rows[:], in_=score_banks[(b, i)][:], mul=1.0 / math.sqrt(D))
            else:
                nc.vector.tensor_scalar_mul(out=rows[:], in0=score_banks[(b, i)][:], scalar1=1.0 / math.sqrt(D))
            g, u = divmod(i, 2)
            rows_out = out_0[b, 2 * P * g : 2 * P * (g + 1), :].rearrange("(p u) j -> p u j", u=2)
            nc.sync.dma_start(out=rows_out[:, u, :], in_=rows[:])

        regroup_weight("v", 0, 0, 84)
        flip_tokens(0, 0, 0)
        flip_tokens(0, 0, 1)
        quantise_weight("v", 0, 0)
        regroup_weight("v", 0, 1, 100)
        quantise_tokens(0, 0)
        quantise_weight("v", 0, 1)
        flip_tokens(0, 1, 0)
        flip_tokens(0, 1, 1)
        spread_bv()
        multiply_values(0, 0, 0)
        regroup_weight("v", 1, 0, 72)
        quantise_tokens(0, 1)
        add_bv(0, 0, 0)
        multiply_values(0, 1, 0)
        regroup_weight("v", 1, 1, 64)
        add_bv(0, 1, 0)
        quantise_weight("v", 1, 0)
        quantise_weight("v", 1, 1)
        for g in range(PASSES):
            for u in range(2):
                flip_tokens(1, g, u)
        multiply_values(0, 0, 1)
        multiply_values(0, 1, 1)
        regroup_weight("q", 0, 0, 40)
        add_bv(0, 0, 1)
        store_values(0, 0)
        add_bv(0, 1, 1)
        store_values(0, 1)
        quantise_tokens(1, 0)
        quantise_tokens(1, 1)
        regroup_weight("q", 0, 1, 40)
        multiply_values(1, 0, 0)
        multiply_values(1, 0, 1)
        quantise_weight("q", 0, 0)
        add_bv(1, 0, 0)
        add_bv(1, 0, 1)
        store_values(1, 0)
        regroup_weight("q", 1, 0, 32)
        quantise_weight("q", 0, 1)
        regroup_weight("q", 1, 1, 32)
        multiply_values(1, 1, 0)
        multiply_values(1, 1, 1)
        regroup_values(0, 0)
        for t in range(PACK):
            project_query_plane(0, 0, t)
        regroup_values(0, 1)
        add_bv(1, 1, 0)
        add_bv(1, 1, 1)
        store_values(1, 1)
        quantise_weight("q", 1, 0)
        quantise_values(0, 0)
        quantise_weight("q", 1, 1)
        for i in range(GROUPS):
            multiply_queries(1, 0, i)
        for t in range(PACK):
            project_query_plane(0, 1, t)
        regroup_values(1, 0)
        regroup_queries(0, 0)
        group_queries(1, 0, 0)
        group_queries(1, 0, 1)
        quantise_queries(0, 0, 0, 4)
        quantise_values(0, 1)
        group_queries(1, 0, 2)
        group_queries(1, 0, 3)
        regroup_queries(0, 1)
        quantise_queries(1, 0, 0, 4)
        quantise_queries(0, 1, 0, 4)
        for i in range(GROUPS):
            multiply_queries(1, 1, i)
        for i in range(GROUPS):
            for g in range(PASSES):
                score_pass(0, i, g)
        regroup_values(1, 1)
        for i in range(GROUPS):
            store_scores(0, i, "scalar")
        quantise_values(1, 0)
        group_queries(1, 1, 0)
        group_queries(1, 1, 1)
        quantise_values(1, 1)
        score_pass(1, 0, 0)
        score_pass(1, 1, 0)
        quantise_queries(1, 1, 0, 1)
        score_pass(1, 0, 1)
        store_scores(1, 0, "scalar")
        group_queries(1, 1, 2)
        score_pass(1, 2, 0)
        quantise_queries(1, 1, 1, 2)
        score_pass(1, 1, 1)
        store_scores(1, 1, "scalar")
        group_queries(1, 1, 3)
        score_pass(1, 3, 0)
        quantise_queries(1, 1, 2, 3)
        score_pass(1, 2, 1)
        quantise_queries(1, 1, 3, 4)
        score_pass(1, 3, 1)
        store_scores(1, 2, "vector")
        store_scores(1, 3, "scalar")
